import numpy as np
import ml_dtypes


def mxq(x, axis, fmt="e4m3"):
    dtype, down = {"e4m3": (ml_dtypes.float8_e4m3fn, 7), "e5m2": (ml_dtypes.float8_e5m2, 14)}[fmt]
    v = np.moveaxis(np.asarray(x, np.float32).astype(ml_dtypes.bfloat16).astype(np.float64), axis, -1)
    blocks = v.reshape(v.shape[:-1] + (-1, 32))
    amax = np.abs(blocks).max(-1, keepdims=True)
    byte = np.maximum(np.where(amax > 0, np.frexp(amax)[1] - 1 + 127, 0) - down, 1)
    scale = np.exp2(byte - 127.0)
    codes = (blocks / scale).astype(np.float32).astype(dtype).astype(np.float64)
    return np.moveaxis((codes * scale).reshape(v.shape), -1, axis)


WIDE = False


def mx_kscale(k):
    if not WIDE:
        return np.ones(k)
    levels = np.array([18, -18])
    if k % 512:
        return np.exp2(np.random.permutation(np.resize(levels, k // 32))).repeat(32)
    a = np.empty((k // 512, 16))
    for p in range(k // 512):
        a[p, :8] = np.random.permutation(np.resize(levels, 8))
        for g in range(8):
            far = levels[np.abs(levels - a[p, g]) >= 10]
            a[p, g + 8] = far[np.random.randint(len(far))]
    return np.exp2(a.ravel()).repeat(32)


BF16 = ml_dtypes.bfloat16


def bf(x):
    return np.asarray(x, np.float32).astype(BF16)


def f64(x):
    return np.asarray(x).astype(np.float64)


B, C, P, NH, NW = 64, 2, 16, 4, 8
D = C * P * P
T = B * NH * NW
QK_SCALE = 1.0


def rel_bias(p):
    i = np.arange(p, dtype=np.float64)
    down = np.exp(-i / (p / 2))[:, None] * np.ones((1, p))
    right = down.T
    br = np.exp(-(i[:, None] + i[None, :]) / (p / 2))
    return np.stack([
        np.rot90(br, 2), np.flip(down, 0), np.rot90(br, 1),
        np.flip(right, 1), np.ones((p, p)), right,
        np.rot90(br, 3), down, br,
    ], axis=0)


def to_patches(v):
    return v.reshape(B, C, NH, P, NW, P).transpose(0, 2, 4, 1, 3, 5)


def neighbour_sum(y, b_qkv):
    full = np.pad(y - b_qkv, ((0, 0), (1, 1), (1, 1), (0, 0))) + b_qkv
    kv = (full[..., D:2 * D] * full[..., 2 * D:]).reshape(B, NH + 2, NW + 2, C, P, P)
    bias = rel_bias(P)
    m = 0.0
    for di in range(3):
        for dj in range(3):
            m = m + bias[3 * di + dj] * kv[:, di:di + NH, dj:dj + NW]
    return m.reshape(B, NH, NW, D)


def setup_inputs():
    s = mx_kscale(T)[::NH * NW].reshape(B, 1, 1, 1)
    u = np.repeat(mx_kscale(3 * D)[::96], 32)
    ui = np.tile(u.reshape(C, P, P), (1, NH, NW))
    x0 = bf(np.random.standard_normal((B, C, NH * P, NW * P)))
    w0 = bf(np.random.standard_normal((3 * D, D)) / np.sqrt(D))
    b = bf(np.random.standard_normal(3 * D) * 0.5)
    e = np.random.randint(-6, 1, (B, 1, NH, NW))
    scale = 0.5 * np.exp2(np.repeat(np.repeat(e, P, axis=2), P, axis=3))
    g = bf(np.random.standard_normal((B, C, NH * P, NW * P)) * scale / s * ui)
    f = to_patches(f64(x0)).reshape(B, NH, NW, D)
    qkv = f @ f64(w0).T + f64(b)
    m = neighbour_sum(qkv, f64(b))
    return {"x": bf(f64(x0) * s), "W_qkv": bf(f64(w0) / np.tile(u, 3)[:, None]), "b_qkv": b,
            "qkv": np.asarray(qkv, np.float32), "m": np.asarray(m, np.float32), "grad_out": g}


def reference(x, W_qkv, b_qkv, qkv, m, grad_out):
    feat = to_patches(f64(x)).reshape(T, D)
    g = to_patches(f64(grad_out))
    y = f64(qkv).reshape(B, NH, NW, 3, C, P, P)
    q, k, v = y[:, :, :, 0], y[:, :, :, 1], y[:, :, :, 2]
    dq = g * f64(m).reshape(B, NH, NW, C, P, P) * QK_SCALE
    h = np.pad(g * q * QK_SCALE, ((0, 0), (1, 1), (1, 1), (0, 0), (0, 0), (0, 0)))
    bias = rel_bias(P)
    n = 0.0
    for di in range(3):
        for dj in range(3):
            n = n + bias[3 * di + dj] * h[:, 2 - di:2 - di + NH, 2 - dj:2 - dj + NW]
    dy = np.concatenate([dq.reshape(T, D), (n * v).reshape(T, D), (n * k).reshape(T, D)], axis=1)
    df = mxq(dy, 1, "e5m2") @ mxq(f64(W_qkv), 0, "e4m3")
    dw = mxq(dy, 0, "e5m2").T @ mxq(feat, 0, "e4m3")
    dx = df.reshape(B, NH, NW, C, P, P).transpose(0, 3, 1, 4, 2, 5).reshape(B, C, NH * P, NW * P)
    return dx, dw

@@ -1,0 +1,426 @@
+import math
+from contextlib import ExitStack
+
+import concourse.mybir as mybir
+from concourse.masks import make_identity
+
+F32 = mybir.dt.float32
+BF16 = mybir.dt.bfloat16
+I32 = mybir.dt.int32
+U32 = mybir.dt.uint32
+U8 = mybir.dt.uint8
+E4M3 = mybir.dt.float8_e4m3fn_x4
+E5M2 = mybir.dt.float8_e5m2_x4
+ALU = mybir.AluOpType
+
+B, CH, PIX, NH, NW = 64, 2, 16, 4, 8
+D = CH * PIX * PIX
+T = B * NH * NW
+P = 128
+GROUPS = 4
+IMGS = B // GROUPS
+CHUNKS = 16
+
+FLOPS = 2 * 2 * T * 3 * D * D
+BYTES = T * D * 2 * 2 + 3 * D * D * 2 + T * 3 * D * 4 + T * D * 4 + T * D * 4 + 3 * D * D * 4
+
+FIRST, LAST = -3, 17
+
+
+def a_before(a):
+    return math.exp(-(15 - a) / 8)
+
+
+def a_after(a):
+    return math.exp(-a / 8)
+
+
+def tile_attentionconv_v_kernel(tc, x, w_qkv, b_qkv, qkv, m, grad_out, out_0, out_1):
+    nc = tc.nc
+    qkv_rows = qkv.rearrange("b i j c -> (b i j) c")
+    m_rows = m.rearrange("b i j c -> (b i j) c")
+
+    with ExitStack() as ctx:
+        const = ctx.enter_context(tc.tile_pool(name="const", bufs=1))
+        loads = ctx.enter_context(tc.tile_pool(name="loads", bufs=2))
+        work = ctx.enter_context(tc.tile_pool(name="work", bufs=2))
+        keep = ctx.enter_context(tc.tile_pool(name="keep", bufs=1))
+        psum = ctx.enter_context(tc.psum_pool(name="psum", bufs=2))
+        ctx.enter_context(tc.manual_schedule())
+
+        q_sb, k_sb, v_sb, m_sb, g_sb, x_sb, w_sb = {}, {}, {}, {}, {}, {}, {}
+
+        def load_rows(rows, cols, g, tag):
+            t = loads.tile([P, 4, D], F32, name=tag, tag=tag)
+            nc.sync.dma_start(out=t[:], in_=rows[512 * g : 512 * g + 512, cols].rearrange("(p t) c -> p t c", t=4))
+            return t
+
+        def load_q(g):
+            q_sb[g] = load_rows(qkv_rows, slice(0, D), g, "q")
+
+        def load_k(g):
+            k_sb[g] = load_rows(qkv_rows, slice(D, 2 * D), g, "k")
+
+        def load_v(g):
+            v_sb[g] = load_rows(qkv_rows, slice(2 * D, 3 * D), g, "v")
+
+        def load_m(g):
+            m_sb[g] = load_rows(m_rows, slice(0, D), g, "m")
+
+        def load_image(src, g, tag, queues):
+            t = loads.tile([P, CH, PIX * NW * PIX], BF16, name=tag, tag=tag)
+            rows = src.rearrange("b c h w -> b c (h w)")
+            for i in range(NH):
+                for jh in range(2):
+                    skip = 64 * jh
+                    n = PIX * NW * PIX - skip
+                    lo = i * PIX * NW * PIX + skip
+                    queues[2 * i + jh].dma_start(
+                        out=t[2 * i + jh : P : 8, :, 0:n],
+                        in_=rows[IMGS * g : IMGS * (g + 1), :, lo : lo + n],
+                    )
+            return t
+
+        def load_g(g):
+            queues = [nc.gpsimd if g == 0 and n >= 6 else nc.sync for n in range(8)]
+            g_sb[g] = load_image(grad_out, g, "g", queues)
+
+        def load_x(g):
+            x_sb[g] = load_image(x, g, "x", [nc.gpsimd] * 8)
+
+        def load_w(a, pool, tag):
+            w_sb[a] = pool.tile([P, 4, D], BF16, name="w_raw", tag=tag, align_bytes=64)
+            nc.sync.dma_start(out=w_sb[a][:], in_=w_qkv[D * a : D * a + D, :].rearrange("(p j) w -> p j w", j=4))
+
+        ident = const.tile([P, P], F32, name="ident")
+        ident_bf = const.tile([P, P], BF16, name="ident_bf")
+        dist = const.tile([P, NH * 4, 8], I32, name="dist")
+        below = const.tile([P, NH * 4, 8], F32, name="below")
+        above = const.tile([P, NH * 4, 8], F32, name="above")
+        vert = const.tile([P, PIX, P], F32, name="vert")
+        lane = const.tile([P, 1], I32, name="lane")
+        bits = const.tile([P, 4], I32, name="bits")
+        factors = const.tile([P, 2, 4], F32, name="factors")
+        pairs = const.tile([P, 2, 2], F32, name="pairs")
+        side = const.tile([P, 2, 1], F32, name="side")
+
+        def constants():
+            nc.gpsimd.iota(dist[:].rearrange("p a b -> p (a b)"), pattern=[[-1, P]], base=0, channel_multiplier=1)
+            nc.gpsimd.iota(lane[:], pattern=[[1, 1]], base=0, channel_multiplier=1)
+            make_identity(nc, ident[:])
+            make_identity(nc, ident_bf[:])
+            nc.vector.memset(below[:], 0.0)
+            nc.vector.memset(above[:], 0.0)
+            nc.vector.tensor_scalar(out=below[:, :, 0:6], in0=dist[:, :, 0:6], scalar1=2.0, scalar2=None, op0=ALU.is_equal)
+            nc.vector.tensor_scalar(out=above[:, :, 2:8], in0=dist[:, :, 2:8], scalar1=-2.0, scalar2=None, op0=ALU.is_equal)
+            for n in range(4):
+                nc.vector.tensor_scalar(out=bits[:, n : n + 1], in0=lane[:], scalar1=n, scalar2=1, op0=ALU.logical_shift_right, op1=ALU.bitwise_and)
+            for n in range(4):
+                step = math.exp(2**n / 8)
+                c = math.exp(-15 / 8) if n == 3 else 1.0
+                nc.vector.tensor_scalar(out=factors[:, 0, n : n + 1], in0=bits[:, n : n + 1], scalar1=(step - 1) * c, scalar2=c, op0=ALU.mult, op1=ALU.add)
+                nc.vector.tensor_scalar(out=factors[:, 1, n : n + 1], in0=bits[:, n : n + 1], scalar1=1 / step - 1, scalar2=1.0, op0=ALU.mult, op1=ALU.add)
+            for r in range(PIX):
+                nc.vector.scalar_tensor_tensor(out=vert[:, r, :], in0=below[:].rearrange("p a b -> p (a b)"), scalar=a_before(r), in1=ident[:], op0=ALU.mult, op1=ALU.add)
+                if r == 1:
+                    nc.vector.tensor_tensor(out=pairs[:], in0=factors[:, :, 0:2], in1=factors[:, :, 2:4], op=ALU.mult)
+                if r == 3:
+                    nc.vector.tensor_tensor(out=side[:], in0=pairs[:, :, 0:1], in1=pairs[:, :, 1:2], op=ALU.mult)
+            for r in range(PIX):
+                nc.vector.scalar_tensor_tensor(out=vert[:, r, :], in0=above[:].rearrange("p a b -> p (a b)"), scalar=a_after(r), in1=vert[:, r, :], op0=ALU.mult, op1=ALU.add)
+
+        h_sb, u_sb, n_sb, t_ps, n_ps = {}, {}, {}, {}, {}
+
+        def product_h(hh):
+            g, half = hh // 2, hh % 2
+            h = work.tile([P, 4, CH, 8, PIX], F32, name="h", tag="h")
+            grad = g_sb[g][:].rearrange("p c (r x) -> p c r x", x=P)
+            for ch in range(CH):
+                lo = 256 * ch + 128 * half
+                nc.vector.tensor_tensor(
+                    out=h[:, :, ch].rearrange("p t r s -> p t r s"),
+                    in0=grad[:, ch, 8 * half : 8 * half + 8, 0:64].rearrange("p r (t s) -> p t r s", t=4),
+                    in1=q_sb[g][:, :, lo : lo + 128].rearrange("p t (r s) -> p t r s", s=PIX),
+                    op=ALU.mult,
+                )
+            h_sb[hh] = h
+
+        def vertical(c):
+            ps = psum.tile([P, 4, CH, 4, PIX], F32, name="u_ps", tag="u", bufs=1)
+            h = h_sb[c // 2]
+            for rr in range(4):
+                r = 4 * (c % 4) + rr
+                nc.tensor.matmul(
+                    ps[:, :, :, rr, :].rearrange("p t c s -> p (t c) s"),
+                    lhsT=vert[:, r, :],
+                    rhs=h[:, :, :, r % 8, :].rearrange("p t c s -> p (t c) s"),
+                    start=True,
+                    stop=True,
+                )
+            u = work.tile([P, 4, P], F32, name="u", tag="u")
+            nc.scalar.copy(out=u[:].rearrange("p t f -> p (t f)"), in_=ps[:].rearrange("p t c r s -> p (t c r s)"))
+            u_sb[c] = u
+
+        def turn_u(c):
+            ps = psum.tile([P, 4, P], F32, name="t_ps", tag="t", bufs=2)
+            for t in range(4):
+                nc.tensor.transpose(ps[:, t, :], u_sb[c][:, t, :], ident[:])
+            n = work.tile([P, 4, P], F32, name="n", tag="n", bufs=3)
+            nc.scalar.copy(out=n[:].rearrange("p t k -> p (t k)"), in_=ps[:].rearrange("p t k -> p (t k)"))
+            t_ps[c], n_sb[c] = ps, n
+
+        def tap(c, which, n_out, n_in, t_out, t_in, across):
+            out, src = n_sb[c], t_ps[c]
+            if across:
+                o = out[:, t_out, :].rearrange("p (k z) -> p k z", z=2)[:, :, n_out]
+                i = src[:, t_in, :].rearrange("p (k z) -> p k z", z=2)[:, :, n_in]
+            else:
+                o = out[:, t_out, :].rearrange("p t k -> p (t k)")
+                i = src[:, t_in, :].rearrange("p t k -> p (t k)")
+            nc.vector.scalar_tensor_tensor(out=o, in0=i, scalar=side[:, which, :], in1=o, op0=ALU.mult, op1=ALU.add)
+
+        def taps_right(c):
+            tap(c, 0, 0, 0, slice(0, 3), slice(1, 4), False)
+            tap(c, 0, 0, 1, 3, 0, True)
+
+        def taps_left(c):
+            tap(c, 1, 0, 0, slice(1, 4), slice(0, 3), False)
+            tap(c, 1, 1, 0, 0, 3, True)
+
+        def turn_n(c):
+            ps = psum.tile([P, 4, P], F32, name="n_ps", tag="n", bufs=2)
+            for t in range(4):
+                nc.tensor.transpose(ps[:, t, :], n_sb[c][:, t, :], ident[:])
+            n_ps[c] = ps
+
+        dy, dy_t = {}, {}
+        tok, feat, wq, xq = {}, {}, {}, {}
+
+        def new_dy(a, g):
+            dy[a, g] = work.tile([P, D, 4], BF16, name="dy%d" % a, tag="dy%d" % a, align_bytes=64)
+
+        def product_kv(c, a):
+            g, quad = c // 4, c % 4
+            if quad == 0:
+                new_dy(a, g)
+            other = v_sb[g] if a == 1 else k_sb[g]
+            nc.vector.tensor_tensor(
+                out=dy[a, g][:].rearrange("p (c q e) t -> p q c e t", c=CH, q=4)[:, quad],
+                in0=n_ps[c][:].rearrange("p t (c e) -> p c e t", c=CH),
+                in1=other[:].rearrange("p t (c q e) -> p q c e t", c=CH, q=4)[:, quad],
+                op=ALU.mult,
+            )
+
+        def product_q(g, n):
+            if n == 0:
+                new_dy(0, g)
+            grad = g_sb[g][:].rearrange("p c (r x) -> p (c r) x", x=P)[:, 8 * n : 8 * n + 8, 0:64]
+            nc.vector.tensor_tensor(
+                out=dy[0, g][:, 128 * n : 128 * n + 128, :].rearrange("p (r s) t -> p r s t", s=PIX),
+                in0=grad.rearrange("p r (t s) -> p r s t", t=4),
+                in1=m_sb[g][:, :, 128 * n : 128 * n + 128].rearrange("p t (r s) -> p r s t", s=PIX),
+                op=ALU.mult,
+            )
+
+        def quantize(src, fmt, name, tag, bufs, pool):
+            codes = pool.tile([P, D], U32, name=name + "_c", tag=tag + "_c", bufs=bufs, align_bytes=64)
+            scales = pool.tile([P, D], U8, name=name + "_s", tag=tag + "_s", bufs=bufs, align_bytes=64)
+            nc.vector.quantize_mx(out=codes[:].bitcast(fmt), scales=scales[:], in_=src[:].rearrange("p a b -> p (a b)"))
+            return codes, scales
+
+        def quantize_tokens(a, g):
+            tok[a, g] = quantize(dy[a, g], E5M2, "tok%d%d" % (a, g), "tok%d%d" % (a, g), 1, keep)
+
+        def turn_dy(a, g, half, engine):
+            ps = psum.tile([P, 2, 4, P], BF16, name="y_ps", tag="y", bufs=2)
+            for tt in range(2):
+                for f in range(4):
+                    nc.tensor.transpose(ps[:, tt, f, :], dy[a, g][:, f:D:4, 2 * half + tt], ident_bf[:])
+            if half == 0:
+                dy_t[a, g] = work.tile([P, D, 4], BF16, name="dy_t", tag="dy_t", bufs=2, align_bytes=64)
+            o = dy_t[a, g][:, 256 * half : 256 * half + 256, :].rearrange("p (t k) f -> p t k f", t=2)
+            i = ps[:].rearrange("p t f k -> p t k f")
+            if engine == 0:
+                nc.scalar.copy(out=o, in_=i)
+            else:
+                nc.vector.tensor_copy(out=o, in_=i)
+
+        def quantize_features(a, g):
+            feat[a, g] = quantize(dy_t[a, g], E5M2, "feat%d" % a, "feat%d" % a, 2, work)
+
+        lace_sb = {}
+
+        def lace(kind, n, quarter):
+            if quarter == 0:
+                lace_sb[kind, n] = work.tile([P, D, 4], BF16, name="laced", tag="laced", bufs=2, align_bytes=64)
+            cols = slice(128 * quarter, 128 * quarter + 128)
+            if kind == "w":
+                nc.scalar.copy(out=lace_sb[kind, n][:, cols, :], in_=w_sb[n][:, :, cols].rearrange("p j w -> p w j"))
+            else:
+                rows = x_sb[n][:].rearrange("p c (r x) -> p (c r) x", x=P)[:, 8 * quarter : 8 * quarter + 8, 0:64]
+                nc.scalar.copy(
+                    out=lace_sb[kind, n][:, cols, :].rearrange("p (r s) t -> p r s t", s=PIX),
+                    in_=rows.rearrange("p r (t s) -> p r s t", t=4),
+                )
+
+        def quantize_laced(kind, n):
+            done = quantize(lace_sb[kind, n], E4M3, "%sq%d" % (kind, n), "%sq%d" % (kind, n), 1, keep)
+            (wq if kind == "w" else xq)[n] = done
+
+        o0_sb = {}
+
+        def mx(ps, left, cols, right, first, last):
+            nc.tensor.matmul_mx(
+                ps[:],
+                lhsT=left[0][:, cols].bitcast(E5M2),
+                lhsT_scale=left[1][:, cols],
+                rhs=right[0][:].bitcast(E4M3),
+                rhs_scale=right[1][:],
+                start=first,
+                stop=last,
+            )
+
+        def empty(out, in_, engine):
+            if engine == 0:
+                nc.scalar.copy(out=out, in_=in_)
+            else:
+                nc.vector.tensor_copy(out=out, in_=in_)
+
+        def product_x(g, t, tag, engine):
+            ps = psum.tile([P, D], F32, name="mx_ps", tag=tag, bufs=(1 if tag in ("u", "out") else 2))
+            for a in range(3):
+                mx(ps, feat[a, g], slice(128 * t, 128 * t + 128), wq[a], a == 0, a == 2)
+            if t == 0:
+                o0_sb[g] = work.tile([P, CH * PIX, 4, PIX], F32, name="o0", tag="o0", bufs=1, align_bytes=64)
+            empty(o0_sb[g][:, :, t, :], ps[:].rearrange("p (r s) -> p r s", s=PIX), engine)
+            if t == 3:
+                o0 = o0_sb[g][:].rearrange("p r t s -> p r (t s)")
+                for i in range(NH):
+                    for jh in range(2):
+                        for ch in range(CH):
+                            nc.sync.dma_start(
+                                out=out_0[IMGS * g : IMGS * (g + 1), ch, PIX * i : PIX * (i + 1), 64 * jh : 64 * jh + 64],
+                                in_=o0[2 * i + jh : P : 8, PIX * ch : PIX * (ch + 1), :],
+                            )
+
+        def product_w(a, mt, tag, engine):
+            ps = psum.tile([P, D], F32, name="mx_ps", tag=tag, bufs=(1 if tag in ("u", "out") else 2))
+            for g in range(GROUPS):
+                mx(ps, tok[a, g], slice(128 * mt, 128 * mt + 128), xq[g], g == 0, g == GROUPS - 1)
+            o1 = work.tile([P, D], F32, name="o1", tag="n", bufs=3)
+            empty(o1[:], ps[:], engine)
+            lo = D * a + 128 * mt
+            nc.sync.dma_start(out=out_1[lo : lo + 128, :], in_=o1[:])
+
+        load_g(0)
+        load_q(0)
+        constants()
+        load_m(0)
+        load_g(1)
+        load_q(1)
+        load_k(0)
+        load_v(0)
+        load_m(1)
+        load_w(0, work, "dy1")
+        load_w(1, work, "dy2")
+        w_sb[2] = work.tile([P, 4, D], BF16, name="w_raw2", tag="o0", bufs=1, align_bytes=64)
+        nc.sync.dma_start(out=w_sb[2][:], in_=w_qkv[2 * D : 3 * D, :].rearrange("(p j) w -> p j w", j=4))
+        load_k(1)
+        load_v(1)
+        load_x(0)
+        load_x(1)
+
+        lacing = {
+            3: [("w", 0, 0), ("w", 0, 1), ("w", 0, 2)],
+            4: [("w", 0, 3), ("w", 1, 0), ("w", 1, 1)],
+            5: [("w", 1, 2), ("w", 1, 3), ("w", 2, 0)],
+            6: [("w", 2, 1), ("w", 2, 2), ("x", 0, 0)],
+            7: [("w", 2, 3), ("x", 0, 1)],
+            8: [("x", 0, 2), ("x", 0, 3)],
+            9: [("x", 1, 0), ("x", 1, 1)],
+            10: [("x", 1, 2), ("x", 1, 3)],
+            11: [("x", 2, 0), ("x", 2, 1)],
+            12: [("x", 2, 2), ("x", 2, 3)],
+            13: [("x", 3, 0), ("x", 3, 1)],
+            14: [("x", 3, 2), ("x", 3, 3)],
+        }
+        laced = {5: ("w", 0), 6: ("w", 1), 8: ("w", 2), 9: ("x", 0), 11: ("x", 1), 13: ("x", 2), 15: ("x", 3)}
+
+        for s in range(FIRST, LAST + 1):
+            g, phase = s // 4, s % 4
+            if 0 <= s + 1 < CHUNKS:
+                turn_u(s + 1)
+            if 0 <= s - 1 < CHUNKS:
+                turn_n(s - 1)
+            if 0 <= s < CHUNKS:
+                taps_right(s)
+            if 0 <= s - 2 < CHUNKS:
+                product_kv(s - 2, 1)
+            if 0 <= s < CHUNKS:
+                taps_left(s)
+            if 0 <= s - 2 < CHUNKS:
+                product_kv(s - 2, 2)
+            if (s + 3) % 2 == 0 and 0 <= s + 3 < CHUNKS:
+                product_h((s + 3) // 2)
+            if 0 <= s + 2 < CHUNKS:
+                vertical(s + 2)
+            if phase == 0 and 0 <= g - 1 < GROUPS:
+                quantize_tokens(0, g - 1)
+                if g >= 2:
+                    quantize_features(1, g - 2)
+                    turn_dy(2, g - 2, 1, 0)
+                turn_dy(0, g - 1, 0, 0)
+            if phase == 1:
+                if 0 <= g - 2 < GROUPS:
+                    quantize_features(2, g - 2)
+                if 0 <= g - 1 < GROUPS:
+                    turn_dy(0, g - 1, 1, 0)
+            if phase == 2 and 0 <= g - 1 < GROUPS - 1:
+                quantize_features(0, g - 1)
+                quantize_tokens(1, g - 1)
+                turn_dy(1, g - 1, 0, 0)
+            if phase == 3 and 0 <= g - 1 < GROUPS - 1:
+                quantize_tokens(2, g - 1)
+                turn_dy(1, g - 1, 1, 0)
+                turn_dy(2, g - 1, 0, 0)
+            if 0 <= s + 2 < CHUNKS:
+                product_q((s + 2) // 4, (s + 2) % 4)
+            if s in laced:
+                quantize_laced(laced[s][0], laced[s][1])
+            for kind, n, quarter in lacing.get(s, []):
+                lace(kind, n, quarter)
+            if s >= 10:
+                product_x((s - 10) // 4, (s - 10) % 4, "out", 0)
+            if phase == 0 and 0 <= g <= 1:
+                load_q(g + 2)
+            if phase == 2 and 0 <= g <= 1:
+                load_m(g + 2)
+                load_g(g + 2)
+            if phase == 1 and 1 <= g <= 2:
+                load_k(g + 1)
+                load_v(g + 1)
+            if s == 8:
+                load_x(2)
+            if s == 10:
+                load_x(3)
+
+        tags = ["u", "out", "t", "t"]
+        quantize_tokens(1, 3)
+        turn_dy(1, 3, 0, 0)
+        quantize_features(0, 3)
+        turn_dy(1, 3, 1, 1)
+        for mt in range(4):
+            product_w(0, mt, tags[mt], mt % 2)
+        quantize_tokens(2, 3)
+        turn_dy(2, 3, 0, 0)
+        turn_dy(2, 3, 1, 1)
+        quantize_features(1, 3)
+        for t in range(4):
+            product_x(2, t, tags[t], t % 2)
+        quantize_features(2, 3)
+        for mt in range(4):
+            product_w(1, mt, tags[mt], mt % 2)
+        for t in range(4):
+            product_x(3, t, tags[t], t % 2)
+        for mt in range(4):
+            product_w(2, mt, tags[mt], mt % 2)

@@ -70,30 +70,29 @@ def tile_attentionconv_v_kernel(tc, x, w_qkv, b_qkv, qkv, m, grad_out, out_0, ou
         def load_image(src, g, tag, queues):
             t = loads.tile([P, CH, PIX * NW * PIX], BF16, name=tag, tag=tag)
             rows = src.rearrange("b c h w -> b c (h w)")
-            for i in range(NH):
-                for jh in range(2):
-                    skip = 64 * jh
-                    n = PIX * NW * PIX - skip
-                    lo = i * PIX * NW * PIX + skip
-                    queues[2 * i + jh].dma_start(
-                        out=t[2 * i + jh : P : 8, :, 0:n],
-                        in_=rows[IMGS * g : IMGS * (g + 1), :, lo : lo + n],
-                    )
+            for place in (0, 4, 1, 5, 2, 6, 3, 7):
+                i, jh = place // 2, place % 2
+                skip = 64 * jh
+                n = PIX * NW * PIX - skip
+                lo = i * PIX * NW * PIX + skip
+                queues[place].dma_start(
+                    out=t[place:P:8, :, 0:n],
+                    in_=rows[IMGS * g : IMGS * (g + 1), :, lo : lo + n],
+                )
             return t
 
         def load_g(g):
-            queues = [nc.gpsimd if g == 0 and n >= 6 else nc.sync for n in range(8)]
+            queues = [nc.gpsimd if g == 0 and n in (3, 7) else nc.sync for n in range(8)]
             g_sb[g] = load_image(grad_out, g, "g", queues)
 
         def load_x(g):
-            x_sb[g] = load_image(x, g, "x", [nc.gpsimd] * 8)
+            x_sb[g] = load_image(x, g, "x", [nc.sync] * 8)
 
         def load_w(a, pool, tag):
             w_sb[a] = pool.tile([P, 4, D], BF16, name="w_raw", tag=tag, align_bytes=64)
             nc.sync.dma_start(out=w_sb[a][:], in_=w_qkv[D * a : D * a + D, :].rearrange("(p j) w -> p j w", j=4))
 
         ident = const.tile([P, P], F32, name="ident")
-        ident_bf = const.tile([P, P], BF16, name="ident_bf")
         dist = const.tile([P, NH * 4, 8], I32, name="dist")
         below = const.tile([P, NH * 4, 8], F32, name="below")
         above = const.tile([P, NH * 4, 8], F32, name="above")
@@ -108,7 +107,6 @@ def tile_attentionconv_v_kernel(tc, x, w_qkv, b_qkv, qkv, m, grad_out, out_0, ou
             nc.gpsimd.iota(dist[:].rearrange("p a b -> p (a b)"), pattern=[[-1, P]], base=0, channel_multiplier=1)
             nc.gpsimd.iota(lane[:], pattern=[[1, 1]], base=0, channel_multiplier=1)
             make_identity(nc, ident[:])
-            make_identity(nc, ident_bf[:])
             nc.vector.memset(below[:], 0.0)
             nc.vector.memset(above[:], 0.0)
             nc.vector.tensor_scalar(out=below[:, :, 0:6], in0=dist[:, :, 0:6], scalar1=2.0, scalar2=None, op0=ALU.is_equal)
@@ -120,13 +118,15 @@ def tile_attentionconv_v_kernel(tc, x, w_qkv, b_qkv, qkv, m, grad_out, out_0, ou
                 c = math.exp(-15 / 8) if n == 3 else 1.0
                 nc.vector.tensor_scalar(out=factors[:, 0, n : n + 1], in0=bits[:, n : n + 1], scalar1=(step - 1) * c, scalar2=c, op0=ALU.mult, op1=ALU.add)
                 nc.vector.tensor_scalar(out=factors[:, 1, n : n + 1], in0=bits[:, n : n + 1], scalar1=1 / step - 1, scalar2=1.0, op0=ALU.mult, op1=ALU.add)
-            for r in range(PIX):
+            nc.vector.tensor_tensor(out=pairs[:], in0=factors[:, :, 0:2], in1=factors[:, :, 2:4], op=ALU.mult)
+            vertical_matrices(0)
+            nc.vector.tensor_tensor(out=side[:], in0=pairs[:, :, 0:1], in1=pairs[:, :, 1:2], op=ALU.mult)
+
+        def vertical_matrices(quad):
+            rows = range(4 * quad, 4 * quad + 4)
+            for r in rows:
                 nc.vector.scalar_tensor_tensor(out=vert[:, r, :], in0=below[:].rearrange("p a b -> p (a b)"), scalar=a_before(r), in1=ident[:], op0=ALU.mult, op1=ALU.add)
-                if r == 1:
-                    nc.vector.tensor_tensor(out=pairs[:], in0=factors[:, :, 0:2], in1=factors[:, :, 2:4], op=ALU.mult)
-                if r == 3:
-                    nc.vector.tensor_tensor(out=side[:], in0=pairs[:, :, 0:1], in1=pairs[:, :, 1:2], op=ALU.mult)
-            for r in range(PIX):
+            for r in rows:
                 nc.vector.scalar_tensor_tensor(out=vert[:, r, :], in0=above[:].rearrange("p a b -> p (a b)"), scalar=a_after(r), in1=vert[:, r, :], op0=ALU.mult, op1=ALU.add)
 
         h_sb, u_sb, n_sb, t_ps, n_ps = {}, {}, {}, {}, {}
@@ -204,21 +204,23 @@ def tile_attentionconv_v_kernel(tc, x, w_qkv, b_qkv, qkv, m, grad_out, out_0, ou
             if quad == 0:
                 new_dy(a, g)
             other = v_sb[g] if a == 1 else k_sb[g]
-            nc.vector.tensor_tensor(
-                out=dy[a, g][:].rearrange("p (c q e) t -> p q c e t", c=CH, q=4)[:, quad],
-                in0=n_ps[c][:].rearrange("p t (c e) -> p c e t", c=CH),
-                in1=other[:].rearrange("p t (c q e) -> p q c e t", c=CH, q=4)[:, quad],
-                op=ALU.mult,
-            )
+            for ch in range(CH):
+                lo = 256 * ch + 64 * quad
+                nc.vector.tensor_tensor(
+                    out=dy[a, g][:, lo : lo + 64, :].rearrange("p (k i) t -> p k t i", i=4),
+                    in0=n_ps[c][:, :, 64 * ch : 64 * ch + 64].rearrange("p t (k i) -> p k t i", i=4),
+                    in1=other[:, :, lo : lo + 64].rearrange("p t (k i) -> p k t i", i=4),
+                    op=ALU.mult,
+                )
 
         def product_q(g, n):
             if n == 0:
                 new_dy(0, g)
-            grad = g_sb[g][:].rearrange("p c (r x) -> p (c r) x", x=P)[:, 8 * n : 8 * n + 8, 0:64]
+            grad = g_sb[g][:].rearrange("p c (r x) -> p (c r) x", x=P)[:, :, 0:64]
             nc.vector.tensor_tensor(
-                out=dy[0, g][:, 128 * n : 128 * n + 128, :].rearrange("p (r s) t -> p r s t", s=PIX),
-                in0=grad.rearrange("p r (t s) -> p r s t", t=4),
-                in1=m_sb[g][:, :, 128 * n : 128 * n + 128].rearrange("p t (r s) -> p r s t", s=PIX),
+                out=dy[0, g][:].rearrange("p (r k i) t -> p k r t i", k=4, i=4)[:, n],
+                in0=grad.rearrange("p r (t k i) -> p k r t i", k=4, i=4)[:, n],
+                in1=m_sb[g][:].rearrange("p t (r k i) -> p k r t i", k=4, i=4)[:, n],
                 op=ALU.mult,
             )
 
@@ -232,14 +234,14 @@ def tile_attentionconv_v_kernel(tc, x, w_qkv, b_qkv, qkv, m, grad_out, out_0, ou
             tok[a, g] = quantize(dy[a, g], E5M2, "tok%d%d" % (a, g), "tok%d%d" % (a, g), 1, keep)
 
         def turn_dy(a, g, half, engine):
-            ps = psum.tile([P, 2, 4, P], BF16, name="y_ps", tag="y", bufs=2)
-            for tt in range(2):
-                for f in range(4):
-                    nc.tensor.transpose(ps[:, tt, f, :], dy[a, g][:, f:D:4, 2 * half + tt], ident_bf[:])
+            ps = psum.tile([P, 4, P], F32, name="y_ps", tag="y", bufs=2)
+            words = dy[a, g][:].rearrange("p e t -> p (e t)").bitcast(F32)
+            for f in range(4):
+                nc.tensor.transpose(ps[:, f, :], words[:, 2 * f + half : 2 * D : 8], ident[:])
             if half == 0:
                 dy_t[a, g] = work.tile([P, D, 4], BF16, name="dy_t", tag="dy_t", bufs=2, align_bytes=64)
-            o = dy_t[a, g][:, 256 * half : 256 * half + 256, :].rearrange("p (t k) f -> p t k f", t=2)
-            i = ps[:].rearrange("p t f k -> p t k f")
+            o = dy_t[a, g][:, 256 * half : 256 * half + 256, :].rearrange("p (z k) f -> p z k f", z=2)
+            i = ps[:].rearrange("p f k -> p (f k)").bitcast(BF16).rearrange("p (f k z) -> p z k f", f=4, z=2)
             if engine == 0:
                 nc.scalar.copy(out=o, in_=i)
             else:
@@ -255,12 +257,15 @@ def tile_attentionconv_v_kernel(tc, x, w_qkv, b_qkv, qkv, m, grad_out, out_0, ou
                 lace_sb[kind, n] = work.tile([P, D, 4], BF16, name="laced", tag="laced", bufs=2, align_bytes=64)
             cols = slice(128 * quarter, 128 * quarter + 128)
             if kind == "w":
-                nc.scalar.copy(out=lace_sb[kind, n][:, cols, :], in_=w_sb[n][:, :, cols].rearrange("p j w -> p w j"))
-            else:
-                rows = x_sb[n][:].rearrange("p c (r x) -> p (c r) x", x=P)[:, 8 * quarter : 8 * quarter + 8, 0:64]
                 nc.scalar.copy(
-                    out=lace_sb[kind, n][:, cols, :].rearrange("p (r s) t -> p r s t", s=PIX),
-                    in_=rows.rearrange("p r (t s) -> p r s t", t=4),
+                    out=lace_sb[kind, n][:, cols, :].rearrange("p (k i) j -> p k j i", i=4),
+                    in_=w_sb[n][:, :, cols].rearrange("p j (k i) -> p k j i", i=4),
+                )
+            else:
+                rows = x_sb[n][:].rearrange("p c (r x) -> p (c r) x", x=P)[:, :, 0:64]
+                nc.scalar.copy(
+                    out=lace_sb[kind, n][:].rearrange("p (r k i) t -> p k r t i", k=4, i=4)[:, quarter],
+                    in_=rows.rearrange("p r (t k i) -> p k r t i", k=4, i=4)[:, quarter],
                 )
 
         def quantize_laced(kind, n):
@@ -290,27 +295,37 @@ def tile_attentionconv_v_kernel(tc, x, w_qkv, b_qkv, qkv, m, grad_out, out_0, ou
             ps = psum.tile([P, D], F32, name="mx_ps", tag=tag, bufs=(1 if tag in ("u", "out") else 2))
             for a in range(3):
                 mx(ps, feat[a, g], slice(128 * t, 128 * t + 128), wq[a], a == 0, a == 2)
-            if t == 0:
+            if t == 0 and g == 0:
                 o0_sb[g] = work.tile([P, CH * PIX, 4, PIX], F32, name="o0", tag="o0", bufs=1, align_bytes=64)
+            elif t == 0:
+                o0_sb[g] = loads.tile([P, CH * PIX, 4, PIX], F32, name="o0", tag=(None, "q", "k", "v")[g])
             empty(o0_sb[g][:, :, t, :], ps[:].rearrange("p (r s) -> p r s", s=PIX), engine)
             if t == 3:
                 o0 = o0_sb[g][:].rearrange("p r t s -> p r (t s)")
-                for i in range(NH):
-                    for jh in range(2):
-                        for ch in range(CH):
-                            nc.sync.dma_start(
-                                out=out_0[IMGS * g : IMGS * (g + 1), ch, PIX * i : PIX * (i + 1), 64 * jh : 64 * jh + 64],
-                                in_=o0[2 * i + jh : P : 8, PIX * ch : PIX * (ch + 1), :],
-                            )
+                for ch in range(CH):
+                    for place in (0, 4, 1, 5, 2, 6, 3, 7):
+                        i, jh = place // 2, place % 2
+                        nc.sync.dma_start(
+                            out=out_0[IMGS * g : IMGS * (g + 1), ch, PIX * i : PIX * (i + 1), 64 * jh : 64 * jh + 64],
+                            in_=o0[place:P:8, PIX * ch : PIX * (ch + 1), :],
+                        )
 
-        def product_w(a, mt, tag, engine):
+        part = {}
+
+        def product_w(a, mt, groups, tag, engine):
             ps = psum.tile([P, D], F32, name="mx_ps", tag=tag, bufs=(1 if tag in ("u", "out") else 2))
-            for g in range(GROUPS):
-                mx(ps, tok[a, g], slice(128 * mt, 128 * mt + 128), xq[g], g == 0, g == GROUPS - 1)
-            o1 = work.tile([P, D], F32, name="o1", tag="n", bufs=3)
-            empty(o1[:], ps[:], engine)
-            lo = D * a + 128 * mt
-            nc.sync.dma_start(out=out_1[lo : lo + 128, :], in_=o1[:])
+            for g in groups:
+                mx(ps, tok[a, g], slice(128 * mt, 128 * mt + 128), xq[g], g == groups[0], g == groups[-1])
+            if a not in part:
+                part[a] = loads.tile([P, 4, D], F32, name="part", tag=("g", "q", "m")[a])
+            o1 = part[a][:, mt, :]
+            if groups[0] == 0:
+                empty(o1, ps[:], engine)
+            else:
+                nc.vector.tensor_tensor(out=o1, in0=ps[:], in1=o1, op=ALU.add)
+            if groups[-1] == GROUPS - 1:
+                lo = D * a + 128 * mt
+                nc.sync.dma_start(out=out_1[lo : lo + 128, :], in_=o1)
 
         load_g(0)
         load_q(0)
@@ -325,26 +340,23 @@ def tile_attentionconv_v_kernel(tc, x, w_qkv, b_qkv, qkv, m, grad_out, out_0, ou
         load_w(1, work, "dy2")
         w_sb[2] = work.tile([P, 4, D], BF16, name="w_raw2", tag="o0", bufs=1, align_bytes=64)
         nc.sync.dma_start(out=w_sb[2][:], in_=w_qkv[2 * D : 3 * D, :].rearrange("(p j) w -> p j w", j=4))
-        load_k(1)
-        load_v(1)
-        load_x(0)
-        load_x(1)
 
         lacing = {
             3: [("w", 0, 0), ("w", 0, 1), ("w", 0, 2)],
             4: [("w", 0, 3), ("w", 1, 0), ("w", 1, 1)],
             5: [("w", 1, 2), ("w", 1, 3), ("w", 2, 0)],
-            6: [("w", 2, 1), ("w", 2, 2), ("x", 0, 0)],
-            7: [("w", 2, 3), ("x", 0, 1)],
-            8: [("x", 0, 2), ("x", 0, 3)],
-            9: [("x", 1, 0), ("x", 1, 1)],
-            10: [("x", 1, 2), ("x", 1, 3)],
-            11: [("x", 2, 0), ("x", 2, 1)],
-            12: [("x", 2, 2), ("x", 2, 3)],
+            6: [("w", 2, 1), ("w", 2, 2)],
+            7: [("w", 2, 3), ("x", 0, 0)],
+            8: [("x", 0, 1), ("x", 0, 2)],
+            9: [("x", 0, 3), ("x", 1, 0)],
+            10: [("x", 1, 1), ("x", 1, 2)],
+            11: [("x", 1, 3), ("x", 2, 0)],
+            12: [("x", 2, 1), ("x", 2, 2), ("x", 2, 3)],
             13: [("x", 3, 0), ("x", 3, 1)],
-            14: [("x", 3, 2), ("x", 3, 3)],
+            14: [("x", 3, 2)],
+            15: [("x", 3, 3)],
         }
-        laced = {5: ("w", 0), 6: ("w", 1), 8: ("w", 2), 9: ("x", 0), 11: ("x", 1), 13: ("x", 2), 15: ("x", 3)}
+        laced = {5: ("w", 0), 6: ("w", 1), 8: ("w", 2), 10: ("x", 0), 12: ("x", 1), 13: ("x", 2), 16: ("x", 3)}
 
         for s in range(FIRST, LAST + 1):
             g, phase = s // 4, s % 4
@@ -362,6 +374,8 @@ def tile_attentionconv_v_kernel(tc, x, w_qkv, b_qkv, qkv, m, grad_out, out_0, ou
                 product_kv(s - 2, 2)
             if (s + 3) % 2 == 0 and 0 <= s + 3 < CHUNKS:
                 product_h((s + 3) // 2)
+            if -2 <= s <= 0:
+                vertical_matrices(s + 3)
             if 0 <= s + 2 < CHUNKS:
                 vertical(s + 2)
             if phase == 0 and 0 <= g - 1 < GROUPS:
@@ -391,36 +405,58 @@ def tile_attentionconv_v_kernel(tc, x, w_qkv, b_qkv, qkv, m, grad_out, out_0, ou
                 lace(kind, n, quarter)
             if s >= 10:
                 product_x((s - 10) // 4, (s - 10) % 4, "out", 0)
-            if phase == 0 and 0 <= g <= 1:
-                load_q(g + 2)
-            if phase == 2 and 0 <= g <= 1:
-                load_m(g + 2)
-                load_g(g + 2)
-            if phase == 1 and 1 <= g <= 2:
-                load_k(g + 1)
-                load_v(g + 1)
-            if s == 8:
+            if s == 14:
+                product_w(1, 0, (0, 1, 2), "u", 0)
+                product_w(1, 1, (0, 1, 2), "u", 0)
+            if s == 15:
+                product_w(1, 2, (0, 1, 2), "u", 0)
+                product_w(1, 3, (0, 1, 2), "u", 0)
+            if s == 16:
+                for n in range(4):
+                    product_w(2, n, (0, 1, 2), ["u", "t", "t", "u"][n], n % 2)
+            if s == 17:
+                for n in range(4):
+                    product_w(0, n, (0, 1, 2, 3), ["u", "t", "t", "u"][n], n % 2)
+            if s == 1:
+                load_q(2)
+                load_g(2)
+                load_k(1)
+                load_v(1)
+                load_m(2)
+                load_x(0)
+            if s == 4:
+                load_q(3)
+            if s == 5:
+                load_k(2)
+                load_v(2)
+                load_g(3)
+                load_m(3)
+                load_x(1)
+            if s == 9:
+                load_k(3)
+                load_v(3)
                 load_x(2)
-            if s == 10:
+            if s == 11:
                 load_x(3)
 
         tags = ["u", "out", "t", "t"]
-        quantize_tokens(1, 3)
+        late = (3,)
         turn_dy(1, 3, 0, 0)
+        quantize_tokens(1, 3)
         quantize_features(0, 3)
         turn_dy(1, 3, 1, 1)
-        for mt in range(4):
-            product_w(0, mt, tags[mt], mt % 2)
-        quantize_tokens(2, 3)
+        for n in range(2):
+            product_x(2, n, tags[n], n % 2)
         turn_dy(2, 3, 0, 0)
+        quantize_tokens(2, 3)
         turn_dy(2, 3, 1, 1)
         quantize_features(1, 3)
-        for t in range(4):
-            product_x(2, t, tags[t], t % 2)
+        for n in range(2, 4):
+            product_x(2, n, tags[n], 0)
         quantize_features(2, 3)
-        for mt in range(4):
-            product_w(1, mt, tags[mt], mt % 2)
-        for t in range(4):
-            product_x(3, t, tags[t], t % 2)
-        for mt in range(4):
-            product_w(2, mt, tags[mt], mt % 2)
+        for n in range(4):
+            product_w(1, n, late, tags[n], 1)
+        for n in range(4):
+            product_w(2, n, late, tags[n], 1)
+        for n in range(4):
+            product_x(3, n, ["n", "n", "t", "t"][n], n % 2)

import math
from contextlib import ExitStack

import concourse.mybir as mybir
from concourse.masks import make_identity

F32 = mybir.dt.float32
BF16 = mybir.dt.bfloat16
I32 = mybir.dt.int32
U32 = mybir.dt.uint32
U8 = mybir.dt.uint8
E4M3 = mybir.dt.float8_e4m3fn_x4
E5M2 = mybir.dt.float8_e5m2_x4
ALU = mybir.AluOpType

B, CH, PIX, NH, NW = 64, 2, 16, 4, 8
D = CH * PIX * PIX
T = B * NH * NW
P = 128
GROUPS = 4
IMGS = B // GROUPS
CHUNKS = 16

FLOPS = 2 * 2 * T * 3 * D * D
BYTES = T * D * 2 * 2 + 3 * D * D * 2 + T * 3 * D * 4 + T * D * 4 + T * D * 4 + 3 * D * D * 4

FIRST, LAST = -3, 17


def a_before(a):
    return math.exp(-(15 - a) / 8)


def a_after(a):
    return math.exp(-a / 8)


def tile_attentionconv_v_kernel(tc, x, w_qkv, b_qkv, qkv, m, grad_out, out_0, out_1):
    nc = tc.nc
    qkv_rows = qkv.rearrange("b i j c -> (b i j) c")
    m_rows = m.rearrange("b i j c -> (b i j) c")

    with ExitStack() as ctx:
        const = ctx.enter_context(tc.tile_pool(name="const", bufs=1))
        loads = ctx.enter_context(tc.tile_pool(name="loads", bufs=2))
        work = ctx.enter_context(tc.tile_pool(name="work", bufs=2))
        keep = ctx.enter_context(tc.tile_pool(name="keep", bufs=1))
        psum = ctx.enter_context(tc.psum_pool(name="psum", bufs=2))
        ctx.enter_context(tc.manual_schedule())

        q_sb, k_sb, v_sb, m_sb, g_sb, x_sb, w_sb = {}, {}, {}, {}, {}, {}, {}

        def load_rows(rows, cols, g, tag):
            t = loads.tile([P, 4, D], F32, name=tag, tag=tag)
            nc.sync.dma_start(out=t[:], in_=rows[512 * g : 512 * g + 512, cols].rearrange("(p t) c -> p t c", t=4))
            return t

        def load_q(g):
            q_sb[g] = load_rows(qkv_rows, slice(0, D), g, "q")

        def load_k(g):
            k_sb[g] = load_rows(qkv_rows, slice(D, 2 * D), g, "k")

        def load_v(g):
            v_sb[g] = load_rows(qkv_rows, slice(2 * D, 3 * D), g, "v")

        def load_m(g):
            m_sb[g] = load_rows(m_rows, slice(0, D), g, "m")

        def load_image(src, g, tag, queues):
            t = loads.tile([P, CH, PIX * NW * PIX], BF16, name=tag, tag=tag)
            rows = src.rearrange("b c h w -> b c (h w)")
            for place in (0, 4, 1, 5, 2, 6, 3, 7):
                i, jh = place // 2, place % 2
                skip = 64 * jh
                n = PIX * NW * PIX - skip
                lo = i * PIX * NW * PIX + skip
                queues[place].dma_start(
                    out=t[place:P:8, :, 0:n],
                    in_=rows[IMGS * g : IMGS * (g + 1), :, lo : lo + n],
                )
            return t

        def load_g(g):
            queues = [nc.gpsimd if g == 0 and n in (3, 7) else nc.sync for n in range(8)]
            g_sb[g] = load_image(grad_out, g, "g", queues)

        def load_x(g):
            x_sb[g] = load_image(x, g, "x", [nc.sync] * 8)

        def load_w(a, pool, tag):
            w_sb[a] = pool.tile([P, 4, D], BF16, name="w_raw", tag=tag, align_bytes=64)
            nc.sync.dma_start(out=w_sb[a][:], in_=w_qkv[D * a : D * a + D, :].rearrange("(p j) w -> p j w", j=4))

        ident = const.tile([P, P], F32, name="ident")
        dist = const.tile([P, NH * 4, 8], I32, name="dist")
        below = const.tile([P, NH * 4, 8], F32, name="below")
        above = const.tile([P, NH * 4, 8], F32, name="above")
        vert = const.tile([P, PIX, P], F32, name="vert")
        lane = const.tile([P, 1], I32, name="lane")
        bits = const.tile([P, 4], I32, name="bits")
        factors = const.tile([P, 2, 4], F32, name="factors")
        pairs = const.tile([P, 2, 2], F32, name="pairs")
        side = const.tile([P, 2, 1], F32, name="side")

        def constants():
            nc.gpsimd.iota(dist[:].rearrange("p a b -> p (a b)"), pattern=[[-1, P]], base=0, channel_multiplier=1)
            nc.gpsimd.iota(lane[:], pattern=[[1, 1]], base=0, channel_multiplier=1)
            make_identity(nc, ident[:])
            nc.vector.memset(below[:], 0.0)
            nc.vector.memset(above[:], 0.0)
            nc.vector.tensor_scalar(out=below[:, :, 0:6], in0=dist[:, :, 0:6], scalar1=2.0, scalar2=None, op0=ALU.is_equal)
            nc.vector.tensor_scalar(out=above[:, :, 2:8], in0=dist[:, :, 2:8], scalar1=-2.0, scalar2=None, op0=ALU.is_equal)
            for n in range(4):
                nc.vector.tensor_scalar(out=bits[:, n : n + 1], in0=lane[:], scalar1=n, scalar2=1, op0=ALU.logical_shift_right, op1=ALU.bitwise_and)
            for n in range(4):
                step = math.exp(2**n / 8)
                c = math.exp(-15 / 8) if n == 3 else 1.0
                nc.vector.tensor_scalar(out=factors[:, 0, n : n + 1], in0=bits[:, n : n + 1], scalar1=(step - 1) * c, scalar2=c, op0=ALU.mult, op1=ALU.add)
                nc.vector.tensor_scalar(out=factors[:, 1, n : n + 1], in0=bits[:, n : n + 1], scalar1=1 / step - 1, scalar2=1.0, op0=ALU.mult, op1=ALU.add)
            nc.vector.tensor_tensor(out=pairs[:], in0=factors[:, :, 0:2], in1=factors[:, :, 2:4], op=ALU.mult)
            vertical_matrices(0)
            nc.vector.tensor_tensor(out=side[:], in0=pairs[:, :, 0:1], in1=pairs[:, :, 1:2], op=ALU.mult)

        def vertical_matrices(quad):
            rows = range(4 * quad, 4 * quad + 4)
            for r in rows:
                nc.vector.scalar_tensor_tensor(out=vert[:, r, :], in0=below[:].rearrange("p a b -> p (a b)"), scalar=a_before(r), in1=ident[:], op0=ALU.mult, op1=ALU.add)
            for r in rows:
                nc.vector.scalar_tensor_tensor(out=vert[:, r, :], in0=above[:].rearrange("p a b -> p (a b)"), scalar=a_after(r), in1=vert[:, r, :], op0=ALU.mult, op1=ALU.add)

        h_sb, u_sb, n_sb, t_ps, n_ps = {}, {}, {}, {}, {}

        def product_h(hh):
            g, half = hh // 2, hh % 2
            h = work.tile([P, 4, CH, 8, PIX], F32, name="h", tag="h")
            grad = g_sb[g][:].rearrange("p c (r x) -> p c r x", x=P)
            for ch in range(CH):
                lo = 256 * ch + 128 * half
                nc.vector.tensor_tensor(
                    out=h[:, :, ch].rearrange("p t r s -> p t r s"),
                    in0=grad[:, ch, 8 * half : 8 * half + 8, 0:64].rearrange("p r (t s) -> p t r s", t=4),
                    in1=q_sb[g][:, :, lo : lo + 128].rearrange("p t (r s) -> p t r s", s=PIX),
                    op=ALU.mult,
                )
            h_sb[hh] = h

        def vertical(c):
            ps = psum.tile([P, 4, CH, 4, PIX], F32, name="u_ps", tag="u", bufs=1)
            h = h_sb[c // 2]
            for rr in range(4):
                r = 4 * (c % 4) + rr
                nc.tensor.matmul(
                    ps[:, :, :, rr, :].rearrange("p t c s -> p (t c) s"),
                    lhsT=vert[:, r, :],
                    rhs=h[:, :, :, r % 8, :].rearrange("p t c s -> p (t c) s"),
                    start=True,
                    stop=True,
                )
            u = work.tile([P, 4, P], F32, name="u", tag="u")
            nc.scalar.copy(out=u[:].rearrange("p t f -> p (t f)"), in_=ps[:].rearrange("p t c r s -> p (t c r s)"))
            u_sb[c] = u

        def turn_u(c):
            ps = psum.tile([P, 4, P], F32, name="t_ps", tag="t", bufs=2)
            for t in range(4):
                nc.tensor.transpose(ps[:, t, :], u_sb[c][:, t, :], ident[:])
            n = work.tile([P, 4, P], F32, name="n", tag="n", bufs=3)
            nc.scalar.copy(out=n[:].rearrange("p t k -> p (t k)"), in_=ps[:].rearrange("p t k -> p (t k)"))
            t_ps[c], n_sb[c] = ps, n

        def tap(c, which, n_out, n_in, t_out, t_in, across):
            out, src = n_sb[c], t_ps[c]
            if across:
                o = out[:, t_out, :].rearrange("p (k z) -> p k z", z=2)[:, :, n_out]
                i = src[:, t_in, :].rearrange("p (k z) -> p k z", z=2)[:, :, n_in]
            else:
                o = out[:, t_out, :].rearrange("p t k -> p (t k)")
                i = src[:, t_in, :].rearrange("p t k -> p (t k)")
            nc.vector.scalar_tensor_tensor(out=o, in0=i, scalar=side[:, which, :], in1=o, op0=ALU.mult, op1=ALU.add)

        def taps_right(c):
            tap(c, 0, 0, 0, slice(0, 3), slice(1, 4), False)
            tap(c, 0, 0, 1, 3, 0, True)

        def taps_left(c):
            tap(c, 1, 0, 0, slice(1, 4), slice(0, 3), False)
            tap(c, 1, 1, 0, 0, 3, True)

        def turn_n(c):
            ps = psum.tile([P, 4, P], F32, name="n_ps", tag="n", bufs=2)
            for t in range(4):
                nc.tensor.transpose(ps[:, t, :], n_sb[c][:, t, :], ident[:])
            n_ps[c] = ps

        dy, dy_t = {}, {}
        tok, feat, wq, xq = {}, {}, {}, {}

        def new_dy(a, g):
            dy[a, g] = work.tile([P, D, 4], BF16, name="dy%d" % a, tag="dy%d" % a, align_bytes=64)

        def product_kv(c, a):
            g, quad = c // 4, c % 4
            if quad == 0:
                new_dy(a, g)
            other = v_sb[g] if a == 1 else k_sb[g]
            for ch in range(CH):
                lo = 256 * ch + 64 * quad
                nc.vector.tensor_tensor(
                    out=dy[a, g][:, lo : lo + 64, :].rearrange("p (k i) t -> p k t i", i=4),
                    in0=n_ps[c][:, :, 64 * ch : 64 * ch + 64].rearrange("p t (k i) -> p k t i", i=4),
                    in1=other[:, :, lo : lo + 64].rearrange("p t (k i) -> p k t i", i=4),
                    op=ALU.mult,
                )

        def product_q(g, n):
            if n == 0:
                new_dy(0, g)
            grad = g_sb[g][:].rearrange("p c (r x) -> p (c r) x", x=P)[:, :, 0:64]
            nc.vector.tensor_tensor(
                out=dy[0, g][:].rearrange("p (r k i) t -> p k r t i", k=4, i=4)[:, n],
                in0=grad.rearrange("p r (t k i) -> p k r t i", k=4, i=4)[:, n],
                in1=m_sb[g][:].rearrange("p t (r k i) -> p k r t i", k=4, i=4)[:, n],
                op=ALU.mult,
            )

        def quantize(src, fmt, name, tag, bufs, pool):
            codes = pool.tile([P, D], U32, name=name + "_c", tag=tag + "_c", bufs=bufs, align_bytes=64)
            scales = pool.tile([P, D], U8, name=name + "_s", tag=tag + "_s", bufs=bufs, align_bytes=64)
            nc.vector.quantize_mx(out=codes[:].bitcast(fmt), scales=scales[:], in_=src[:].rearrange("p a b -> p (a b)"))
            return codes, scales

        def quantize_tokens(a, g):
            tok[a, g] = quantize(dy[a, g], E5M2, "tok%d%d" % (a, g), "tok%d%d" % (a, g), 1, keep)

        def turn_dy(a, g, half, engine):
            ps = psum.tile([P, 4, P], F32, name="y_ps", tag="y", bufs=2)
            words = dy[a, g][:].rearrange("p e t -> p (e t)").bitcast(F32)
            for f in range(4):
                nc.tensor.transpose(ps[:, f, :], words[:, 2 * f + half : 2 * D : 8], ident[:])
            if half == 0:
                dy_t[a, g] = work.tile([P, D, 4], BF16, name="dy_t", tag="dy_t", bufs=2, align_bytes=64)
            o = dy_t[a, g][:, 256 * half : 256 * half + 256, :].rearrange("p (z k) f -> p z k f", z=2)
            i = ps[:].rearrange("p f k -> p (f k)").bitcast(BF16).rearrange("p (f k z) -> p z k f", f=4, z=2)
            if engine == 0:
                nc.scalar.copy(out=o, in_=i)
            else:
                nc.vector.tensor_copy(out=o, in_=i)

        def quantize_features(a, g):
            feat[a, g] = quantize(dy_t[a, g], E5M2, "feat%d" % a, "feat%d" % a, 2, work)

        lace_sb = {}

        def lace(kind, n, quarter):
            if quarter == 0:
                lace_sb[kind, n] = work.tile([P, D, 4], BF16, name="laced", tag="laced", bufs=2, align_bytes=64)
            cols = slice(128 * quarter, 128 * quarter + 128)
            if kind == "w":
                nc.scalar.copy(
                    out=lace_sb[kind, n][:, cols, :].rearrange("p (k i) j -> p k j i", i=4),
                    in_=w_sb[n][:, :, cols].rearrange("p j (k i) -> p k j i", i=4),
                )
            else:
                rows = x_sb[n][:].rearrange("p c (r x) -> p (c r) x", x=P)[:, :, 0:64]
                nc.scalar.copy(
                    out=lace_sb[kind, n][:].rearrange("p (r k i) t -> p k r t i", k=4, i=4)[:, quarter],
                    in_=rows.rearrange("p r (t k i) -> p k r t i", k=4, i=4)[:, quarter],
                )

        def quantize_laced(kind, n):
            done = quantize(lace_sb[kind, n], E4M3, "%sq%d" % (kind, n), "%sq%d" % (kind, n), 1, keep)
            (wq if kind == "w" else xq)[n] = done

        o0_sb = {}

        def mx(ps, left, cols, right, first, last):
            nc.tensor.matmul_mx(
                ps[:],
                lhsT=left[0][:, cols].bitcast(E5M2),
                lhsT_scale=left[1][:, cols],
                rhs=right[0][:].bitcast(E4M3),
                rhs_scale=right[1][:],
                start=first,
                stop=last,
            )

        def empty(out, in_, engine):
            if engine == 0:
                nc.scalar.copy(out=out, in_=in_)
            else:
                nc.vector.tensor_copy(out=out, in_=in_)

        def product_x(g, t, tag, engine):
            ps = psum.tile([P, D], F32, name="mx_ps", tag=tag, bufs=(1 if tag in ("u", "out") else 2))
            for a in range(3):
                mx(ps, feat[a, g], slice(128 * t, 128 * t + 128), wq[a], a == 0, a == 2)
            if t == 0 and g == 0:
                o0_sb[g] = work.tile([P, CH * PIX, 4, PIX], F32, name="o0", tag="o0", bufs=1, align_bytes=64)
            elif t == 0:
                o0_sb[g] = loads.tile([P, CH * PIX, 4, PIX], F32, name="o0", tag=(None, "q", "k", "v")[g])
            empty(o0_sb[g][:, :, t, :], ps[:].rearrange("p (r s) -> p r s", s=PIX), engine)
            if t == 3:
                o0 = o0_sb[g][:].rearrange("p r t s -> p r (t s)")
                for ch in range(CH):
                    for place in (0, 4, 1, 5, 2, 6, 3, 7):
                        i, jh = place // 2, place % 2
                        nc.sync.dma_start(
                            out=out_0[IMGS * g : IMGS * (g + 1), ch, PIX * i : PIX * (i + 1), 64 * jh : 64 * jh + 64],
                            in_=o0[place:P:8, PIX * ch : PIX * (ch + 1), :],
                        )

        part = {}

        def product_w(a, mt, groups, tag, engine):
            ps = psum.tile([P, D], F32, name="mx_ps", tag=tag, bufs=(1 if tag in ("u", "out") else 2))
            for g in groups:
                mx(ps, tok[a, g], slice(128 * mt, 128 * mt + 128), xq[g], g == groups[0], g == groups[-1])
            if a not in part:
                part[a] = loads.tile([P, 4, D], F32, name="part", tag=("g", "q", "m")[a])
            o1 = part[a][:, mt, :]
            if groups[0] == 0:
                empty(o1, ps[:], engine)
            else:
                nc.vector.tensor_tensor(out=o1, in0=ps[:], in1=o1, op=ALU.add)
            if groups[-1] == GROUPS - 1:
                lo = D * a + 128 * mt
                nc.sync.dma_start(out=out_1[lo : lo + 128, :], in_=o1)

        load_g(0)
        load_q(0)
        constants()
        load_m(0)
        load_g(1)
        load_q(1)
        load_k(0)
        load_v(0)
        load_m(1)
        load_w(0, work, "dy1")
        load_w(1, work, "dy2")
        w_sb[2] = work.tile([P, 4, D], BF16, name="w_raw2", tag="o0", bufs=1, align_bytes=64)
        nc.sync.dma_start(out=w_sb[2][:], in_=w_qkv[2 * D : 3 * D, :].rearrange("(p j) w -> p j w", j=4))

        lacing = {
            3: [("w", 0, 0), ("w", 0, 1), ("w", 0, 2)],
            4: [("w", 0, 3), ("w", 1, 0), ("w", 1, 1)],
            5: [("w", 1, 2), ("w", 1, 3), ("w", 2, 0)],
            6: [("w", 2, 1), ("w", 2, 2)],
            7: [("w", 2, 3), ("x", 0, 0)],
            8: [("x", 0, 1), ("x", 0, 2)],
            9: [("x", 0, 3), ("x", 1, 0)],
            10: [("x", 1, 1), ("x", 1, 2)],
            11: [("x", 1, 3), ("x", 2, 0)],
            12: [("x", 2, 1), ("x", 2, 2), ("x", 2, 3)],
            13: [("x", 3, 0), ("x", 3, 1)],
            14: [("x", 3, 2)],
            15: [("x", 3, 3)],
        }
        laced = {5: ("w", 0), 6: ("w", 1), 8: ("w", 2), 10: ("x", 0), 12: ("x", 1), 13: ("x", 2), 16: ("x", 3)}

        for s in range(FIRST, LAST + 1):
            g, phase = s // 4, s % 4
            if 0 <= s + 1 < CHUNKS:
                turn_u(s + 1)
            if 0 <= s - 1 < CHUNKS:
                turn_n(s - 1)
            if 0 <= s < CHUNKS:
                taps_right(s)
            if 0 <= s - 2 < CHUNKS:
                product_kv(s - 2, 1)
            if 0 <= s < CHUNKS:
                taps_left(s)
            if 0 <= s - 2 < CHUNKS:
                product_kv(s - 2, 2)
            if (s + 3) % 2 == 0 and 0 <= s + 3 < CHUNKS:
                product_h((s + 3) // 2)
            if -2 <= s <= 0:
                vertical_matrices(s + 3)
            if 0 <= s + 2 < CHUNKS:
                vertical(s + 2)
            if phase == 0 and 0 <= g - 1 < GROUPS:
                quantize_tokens(0, g - 1)
                if g >= 2:
                    quantize_features(1, g - 2)
                    turn_dy(2, g - 2, 1, 0)
                turn_dy(0, g - 1, 0, 0)
            if phase == 1:
                if 0 <= g - 2 < GROUPS:
                    quantize_features(2, g - 2)
                if 0 <= g - 1 < GROUPS:
                    turn_dy(0, g - 1, 1, 0)
            if phase == 2 and 0 <= g - 1 < GROUPS - 1:
                quantize_features(0, g - 1)
                quantize_tokens(1, g - 1)
                turn_dy(1, g - 1, 0, 0)
            if phase == 3 and 0 <= g - 1 < GROUPS - 1:
                quantize_tokens(2, g - 1)
                turn_dy(1, g - 1, 1, 0)
                turn_dy(2, g - 1, 0, 0)
            if 0 <= s + 2 < CHUNKS:
                product_q((s + 2) // 4, (s + 2) % 4)
            if s in laced:
                quantize_laced(laced[s][0], laced[s][1])
            for kind, n, quarter in lacing.get(s, []):
                lace(kind, n, quarter)
            if s >= 10:
                product_x((s - 10) // 4, (s - 10) % 4, "out", 0)
            if s == 14:
                product_w(1, 0, (0, 1, 2), "u", 0)
                product_w(1, 1, (0, 1, 2), "u", 0)
            if s == 15:
                product_w(1, 2, (0, 1, 2), "u", 0)
                product_w(1, 3, (0, 1, 2), "u", 0)
            if s == 16:
                for n in range(4):
                    product_w(2, n, (0, 1, 2), ["u", "t", "t", "u"][n], n % 2)
            if s == 17:
                for n in range(4):
                    product_w(0, n, (0, 1, 2, 3), ["u", "t", "t", "u"][n], n % 2)
            if s == 1:
                load_q(2)
                load_g(2)
                load_k(1)
                load_v(1)
                load_m(2)
                load_x(0)
            if s == 4:
                load_q(3)
            if s == 5:
                load_k(2)
                load_v(2)
                load_g(3)
                load_m(3)
                load_x(1)
            if s == 9:
                load_k(3)
                load_v(3)
                load_x(2)
            if s == 11:
                load_x(3)

        tags = ["u", "out", "t", "t"]
        late = (3,)
        turn_dy(1, 3, 0, 0)
        quantize_tokens(1, 3)
        quantize_features(0, 3)
        turn_dy(1, 3, 1, 1)
        for n in range(2):
            product_x(2, n, tags[n], n % 2)
        turn_dy(2, 3, 0, 0)
        quantize_tokens(2, 3)
        turn_dy(2, 3, 1, 1)
        quantize_features(1, 3)
        for n in range(2, 4):
            product_x(2, n, tags[n], 0)
        quantize_features(2, 3)
        for n in range(4):
            product_w(1, n, late, tags[n], 1)
        for n in range(4):
            product_w(2, n, late, tags[n], 1)
        for n in range(4):
            product_x(3, n, ["n", "n", "t", "t"][n], n % 2)
